import numpy as np
import ml_dtypes


def mxq(x, axis, fmt="e4m3"):
    dtype, down = {"e4m3": (ml_dtypes.float8_e4m3fn, 7), "e5m2": (ml_dtypes.float8_e5m2, 14)}[fmt]
    v = np.moveaxis(np.asarray(x, np.float32).astype(ml_dtypes.bfloat16).astype(np.float64), axis, -1)
    blocks = v.reshape(v.shape[:-1] + (-1, 32))
    amax = np.abs(blocks).max(-1, keepdims=True)
    byte = np.maximum(np.where(amax > 0, np.frexp(amax)[1] - 1 + 127, 0) - down, 1)
    scale = np.exp2(byte - 127.0)
    codes = (blocks / scale).astype(np.float32).astype(dtype).astype(np.float64)
    return np.moveaxis((codes * scale).reshape(v.shape), -1, axis)


WIDE = False


def mx_kscale(k):
    if not WIDE:
        return np.ones(k)
    levels = np.array([10, -10, 5, -5, 0])
    a = np.random.permutation(np.resize(levels, k // 512 * 4)).reshape(k // 512, 4)
    idx = np.arange(k)
    return np.exp2(a[idx // 512, idx % 128 // 32])


BF16 = ml_dtypes.bfloat16


def bf(x):
    return np.asarray(x, np.float32).astype(BF16)


def f64(x):
    return np.asarray(x).astype(np.float64)


B, N, G, C_IN, C_OUT, D = 8, 1024, 255, 2, 2, 128
F = (G + 1) * C_IN


def laplacian_with_self_loop(adj):
    m = adj + np.eye(adj.shape[0])
    d = m.sum(1) ** -0.5
    return (m * d[None, :]).T * d[None, :]


def setup_inputs():
    s = mx_kscale(N)
    t = mx_kscale(F)
    a = 0.25 * np.sqrt(N)
    lap = laplacian_with_self_loop(np.random.random_sample((N, N)))
    return {"x": bf(np.random.standard_normal((B, N, C_IN)) * a / s[None, :, None] * t[None, None, :C_IN]),
            "h": bf(np.random.standard_normal((B, N, G * C_IN)) * a / s[None, :, None] * t[None, None, C_IN:]),
            "laplacian": bf(lap * s[None, :]),
            "weights": bf(np.random.standard_normal((G + 1, D, C_IN, C_OUT)) * 3.0 / np.sqrt(F) / t.reshape(G + 1, C_IN)[:, None, :, None]),
            "biases": bf(np.random.standard_normal((D, C_OUT)) * 0.1)}


def reference(x, h, laplacian, weights, biases):
    xh = np.concatenate([f64(x)[:, :, None, :], f64(h).reshape(B, N, G, C_IN)], axis=2)
    ax = mxq(f64(laplacian), 1, "e4m3") @ mxq(xh.reshape(B, N, F), 1, "e4m3")
    w = f64(weights).transpose(0, 2, 1, 3).reshape(F, D * C_OUT)
    out = (mxq(ax, 2, "e4m3") @ mxq(w, 0, "e4m3")) + f64(biases).reshape(D * C_OUT)
    return out.reshape(B, N * D, C_OUT)

@@ -1,0 +1,227 @@
+from contextlib import ExitStack
+
+import concourse.mybir as mybir
+from concourse.masks import make_identity
+
+BF16 = mybir.dt.bfloat16
+F32 = mybir.dt.float32
+U32 = mybir.dt.uint32
+U8 = mybir.dt.uint8
+FP8X4 = mybir.dt.float8_e4m3fn_x4
+ADD = mybir.AluOpType.add
+
+P = 128
+B = 8
+N = 1024
+F = 512
+H = 510
+DO = 256
+G = 2
+HP = 2048
+MT = 8
+FS = 160
+
+FLOPS = 2 * B * N * N * F + 2 * B * N * F * DO
+
+
+def regroup(copy, dst, src, run):
+    copy(
+        out=dst.rearrange("p (c i) j -> p c j i", i=run),
+        in_=src.rearrange("p j (c i) -> p c j i", i=run),
+    )
+
+
+def tile_tgcngraphconvolution_pa_t_kernel(tc, x, h, laplacian, weights, biases, out):
+    nc = tc.nc
+    with ExitStack() as ctx:
+        const = ctx.enter_context(tc.tile_pool(name="const", bufs=1))
+        hpool = ctx.enter_context(tc.tile_pool(name="hpool", bufs=8))
+        lpool = ctx.enter_context(tc.tile_pool(name="lpool", bufs=4))
+        lgpool = ctx.enter_context(tc.tile_pool(name="lgpool", bufs=3))
+        xpool = ctx.enter_context(tc.tile_pool(name="xpool", bufs=3))
+        apool = ctx.enter_context(tc.tile_pool(name="apool", bufs=4))
+        opool = ctx.enter_context(tc.tile_pool(name="opool", bufs=6))
+        psa = ctx.enter_context(tc.psum_pool(name="psa", bufs=6))
+        pso = ctx.enter_context(tc.psum_pool(name="pso", bufs=2))
+
+        h_v = h.rearrange("b (a p r) f -> b p a (r f)", a=4, r=2)
+        x_v = x.rearrange("b (a p r) c -> p b a (r c)", a=4, r=2)
+        lap_v = laplacian.rearrange("(r i) n -> r (i n)", i=MT)
+        w_v = weights.rearrange("(a k) d c o -> k a (d c o)", a=2)
+        b_v = biases.rearrange("(a d) o -> a (d o)", a=1)
+        out_v = out.rearrange("b (p r) o -> b p (r o)", p=P)
+
+        xraw = const.tile([P, B * 16], BF16, name="xraw")
+        xr = xraw[:].rearrange("p (b a s) -> p b a s", b=B, a=4)
+        nc.scalar.dma_start(out=xr[:, 0:1], in_=x_v[:, 0:1])
+        wraw = const.tile([P, 1024], BF16, name="wraw")
+        nc.scalar.dma_start(out=wraw[:].rearrange("k (a r) -> k a r", a=2), in_=w_v)
+        brow = const.tile([P, DO], BF16, name="brow")
+        nc.vector.memset(brow[:], 0.0)
+        nc.scalar.dma_start(out=brow[0:1, :], in_=b_v)
+
+        hraws = []
+        lraws = []
+
+        def load_h(b):
+            hraw = hpool.tile([P, G * HP], BF16, tag="hraw", name="hraw")
+            for g in range(G):
+                nc.sync.dma_start(
+                    out=hraw[:, HP * g : HP * g + 4 * H].rearrange("p (a r) -> p a r", a=2),
+                    in_=h_v[b][:, 2 * g : 2 * g + 2, :],
+                )
+            hraws.append(hraw)
+
+        load_h(0)
+        for i2 in range(MT // 2):
+            lraw = lpool.tile([P, 2 * N], BF16, tag="lraw", name="lraw")
+            nc.sync.dma_start(out=lraw[:], in_=lap_v[:, 2 * N * i2 : 2 * N * i2 + 2 * N])
+            lraws.append(lraw)
+        nc.sync.dma_start(out=xr[:, 1:B], in_=x_v[:, 1:B])
+        for b in range(1, B):
+            load_h(b)
+
+        ident = const.tile([P, P], F32, name="ident")
+        make_identity(nc, ident[:])
+        perm = const.tile([P, 4 * P], BF16, name="perm")
+        nc.vector.memset(perm[:], 0.0)
+        perm_w = perm[:].rearrange("k (s c i e) -> k s c i e", s=2, c=2, e=2)
+        for c in range(2):
+            nc.vector.tensor_copy(
+                out=perm_w[:, :, c, :, c], in_=ident[:].rearrange("k (s i) -> k s i", s=2)
+            )
+        perm_r = perm[:].rearrange("k (s c q) -> k s c q", s=2, c=2)
+        ones = const.tile([P, P], BF16, name="ones")
+        nc.vector.memset(ones[:], 1.0)
+
+        wr = wraw[:].rearrange("k (a d c o) -> k a d c o", a=2, c=2, o=2)
+        gw = const.tile([P, 4 * DO], BF16, name="gw", align_bytes=64)
+        gw_v = gw[:].rearrange("p (n t) -> p n t", t=4)
+        for a in range(2):
+            wps = pso.tile([P, 512], F32, tag="o", name="wps")
+            for s in range(2):
+                for c in range(2):
+                    nc.tensor.matmul(
+                        out=wps[:, DO * s : DO * s + DO].rearrange("p (d o) -> p d o", o=2),
+                        lhsT=perm_r[:, s, c, :],
+                        rhs=wr[:, a, :, c, :],
+                        start=(c == 0),
+                        stop=(c == 1),
+                    )
+            nc.scalar.copy(
+                out=gw_v[:, :, 2 * a : 2 * a + 2], in_=wps[:].rearrange("p (t n) -> p n t", t=2)
+            )
+        wcodes = const.tile([P, DO], U32, name="wcodes", align_bytes=64)
+        wplane = const.tile([P, DO], U8, name="wplane", align_bytes=64)
+        nc.vector.quantize_mx(out=wcodes[:].bitcast(FP8X4), scales=wplane[:], in_=gw[:])
+
+        bps = pso.tile([P, 512], F32, tag="o", name="bps")
+        for s in range(2):
+            nc.tensor.matmul(
+                out=bps[:, DO * s : DO * s + DO], lhsT=ones[:], rhs=brow[:], start=True, stop=True
+            )
+        bias2 = const.tile([P, 512], F32, name="bias2")
+        nc.scalar.copy(out=bias2[:], in_=bps[:])
+
+        xv = xraw[:].rearrange("p (b g j c) -> p b g j c", b=B, g=G, j=4)
+        xq = {}
+
+        def xh_prep(b):
+            hv = hraws[b][:].rearrange("p (g r) -> p g r", g=G)[:, :, 0 : 4 * H].rearrange(
+                "p g (j f) -> p g j f", j=4
+            )
+            xg = xpool.tile([P, G * F * 4], BF16, tag="xg", name="xg", align_bytes=64)
+            xg_v = xg[:].rearrange("p (g f j) -> p g f j", g=G, j=4)
+            xcodes = xpool.tile([P, G * F], U32, tag="xcodes", name="xcodes", align_bytes=64)
+            xplane = xpool.tile([P, G * F], U8, tag="xplane", name="xplane", align_bytes=64)
+            nc.scalar.copy(out=xg_v[:, :, 0:2, :], in_=xv[:, b].rearrange("p g j c -> p g c j"))
+            for g in range(G):
+                regroup(nc.scalar.copy, xg_v[:, g, 2:FS, :], hv[:, g, :, 0 : FS - 2], 2)
+                regroup(nc.vector.tensor_copy, xg_v[:, g, FS:F, :], hv[:, g, :, FS - 2 : H], 4)
+            for g in range(G):
+                nc.vector.quantize_mx(
+                    out=xcodes[:, F * g : F * g + F].bitcast(FP8X4),
+                    scales=xplane[:, F * g : F * g + F],
+                    in_=xg[:, 4 * F * g : 4 * F * g + 4 * F],
+                )
+            xq[b] = (xcodes, xplane)
+
+        xh_prep(0)
+
+        lcodes = const.tile([P, MT * G * P], U32, name="lcodes", align_bytes=64)
+        lplane = const.tile([P, MT * G * P], U8, name="lplane", align_bytes=64)
+        for i in range(MT):
+            lw = lraws[i // 2][:].bitcast(F32)[:, 512 * (i % 2) : 512 * (i % 2) + 512]
+            lps = psa.tile([P, 512], F32, tag="a", name="lps")
+            for q in range(4):
+                nc.tensor.transpose(lps[:, P * q : P * q + P], lw[:, P * q : P * q + P], ident[:])
+            lgrp = lgpool.tile([P, N], BF16, tag="lgrp", name="lgrp", align_bytes=64)
+            nc.scalar.copy(
+                out=lgrp[:].bitcast(F32).rearrange("p (g m u) -> p g m u", g=G, u=2),
+                in_=lps[:].rearrange("p (g u m) -> p g m u", g=G, u=2),
+            )
+            nc.vector.quantize_mx(
+                out=lcodes[:, 256 * i : 256 * i + 256].bitcast(FP8X4),
+                scales=lplane[:, 256 * i : 256 * i + 256],
+                in_=lgrp[:],
+            )
+
+        aq = {}
+
+        def step2(b, hf):
+            xcodes, xplane = xq[b]
+            ag = apool.tile([P, 2048], BF16, tag="ag", name="ag", align_bytes=64)
+            for ii in range(4):
+                i = 4 * hf + ii
+                aps = psa.tile([P, 512], F32, tag="a", name="aps")
+                for t in range(4):
+                    for g in range(G):
+                        xs = slice(F * g + P * t, F * g + P * t + P)
+                        ls = slice(256 * i + P * g, 256 * i + P * g + P)
+                        nc.tensor.matmul_mx(
+                            out=aps[:, P * t : P * t + P],
+                            lhsT=xcodes[:, xs].bitcast(FP8X4),
+                            lhsT_scale=xplane[:, xs],
+                            rhs=lcodes[:, ls].bitcast(FP8X4),
+                            rhs_scale=lplane[:, ls],
+                            start=(g == 0),
+                            stop=(g == G - 1),
+                        )
+                nc.scalar.copy(
+                    out=ag[:, 512 * ii : 512 * ii + 512].rearrange("p (m t) -> p m t", t=4),
+                    in_=aps[:].rearrange("p (t m) -> p m t", t=4),
+                )
+            acodes = apool.tile([P, 512], U32, tag="acodes", name="acodes", align_bytes=64)
+            aplane = apool.tile([P, 512], U8, tag="aplane", name="aplane", align_bytes=64)
+            nc.vector.quantize_mx(out=acodes[:].bitcast(FP8X4), scales=aplane[:], in_=ag[:])
+            aq[(b, hf)] = (acodes, aplane)
+
+        def step3(b, hf):
+            acodes, aplane = aq[(b, hf)]
+            osb = opool.tile([P, 1024], F32, tag="osb", name="osb")
+            for pr in range(2):
+                ops = pso.tile([P, 512], F32, tag="o", name="ops")
+                for s in range(2):
+                    cs = slice(P * (2 * pr + s), P * (2 * pr + s) + P)
+                    nc.tensor.matmul_mx(
+                        out=ops[:, DO * s : DO * s + DO],
+                        lhsT=acodes[:, cs].bitcast(FP8X4),
+                        lhsT_scale=aplane[:, cs],
+                        rhs=wcodes[:].bitcast(FP8X4),
+                        rhs_scale=wplane[:],
+                        start=True,
+                        stop=True,
+                    )
+                nc.vector.tensor_tensor(
+                    out=osb[:, 512 * pr : 512 * pr + 512], in0=ops[:], in1=bias2[:], op=ADD
+                )
+            nc.sync.dma_start(out=out_v[b][:, 1024 * hf : 1024 * hf + 1024], in_=osb[:])
+
+        halves = [(b, hf) for b in range(B) for hf in range(2)]
+        for k, (b, hf) in enumerate(halves):
+            step2(b, hf)
+            if hf == 0 and b + 1 < B:
+                xh_prep(b + 1)
+            if k >= 1:
+                step3(*halves[k - 1])
+        step3(*halves[-1])

@@ -19,7 +19,10 @@ DO = 256
 G = 2
 HP = 2048
 MT = 8
-FS = 160
+NA = 5
+NO = 3
+NH = 2 * B
+FSQ = [176,176,32,32,96,96,176,176,176,176,176,176,176,176,176,176]
 
 FLOPS = 2 * B * N * N * F + 2 * B * N * F * DO
 
@@ -41,8 +44,21 @@ def tile_tgcngraphconvolution_pa_t_kernel(tc, x, h, laplacian, weights, biases, 
         xpool = ctx.enter_context(tc.tile_pool(name="xpool", bufs=3))
         apool = ctx.enter_context(tc.tile_pool(name="apool", bufs=4))
         opool = ctx.enter_context(tc.tile_pool(name="opool", bufs=6))
-        psa = ctx.enter_context(tc.psum_pool(name="psa", bufs=6))
-        pso = ctx.enter_context(tc.psum_pool(name="pso", bufs=2))
+        psa = ctx.enter_context(tc.psum_pool(name="psa", bufs=1))
+        pso = ctx.enter_context(tc.psum_pool(name="pso", bufs=1))
+        ctx.enter_context(tc.manual_schedule())
+
+        count = {"a": 0, "o": 0}
+
+        def a_bank():
+            n = count["a"]
+            count["a"] = n + 1
+            return psa.tile([P, 512], F32, tag="a%d" % (n % NA), name="a%d" % (n % NA))
+
+        def o_bank():
+            n = count["o"]
+            count["o"] = n + 1
+            return pso.tile([P, 512], F32, tag="o%d" % (n % NO), name="o%d" % (n % NO))
 
         h_v = h.rearrange("b (a p r) f -> b p a (r f)", a=4, r=2)
         x_v = x.rearrange("b (a p r) c -> p b a (r c)", a=4, r=2)
@@ -53,7 +69,7 @@ def tile_tgcngraphconvolution_pa_t_kernel(tc, x, h, laplacian, weights, biases, 
 
         xraw = const.tile([P, B * 16], BF16, name="xraw")
         xr = xraw[:].rearrange("p (b a s) -> p b a s", b=B, a=4)
-        nc.scalar.dma_start(out=xr[:, 0:1], in_=x_v[:, 0:1])
+        nc.scalar.dma_start(out=xr[:, 0:2], in_=x_v[:, 0:2])
         wraw = const.tile([P, 1024], BF16, name="wraw")
         nc.scalar.dma_start(out=wraw[:].rearrange("k (a r) -> k a r", a=2), in_=w_v)
         brow = const.tile([P, DO], BF16, name="brow")
@@ -77,8 +93,9 @@ def tile_tgcngraphconvolution_pa_t_kernel(tc, x, h, laplacian, weights, biases, 
             lraw = lpool.tile([P, 2 * N], BF16, tag="lraw", name="lraw")
             nc.sync.dma_start(out=lraw[:], in_=lap_v[:, 2 * N * i2 : 2 * N * i2 + 2 * N])
             lraws.append(lraw)
-        nc.sync.dma_start(out=xr[:, 1:B], in_=x_v[:, 1:B])
-        for b in range(1, B):
+        load_h(1)
+        nc.sync.dma_start(out=xr[:, 2:B], in_=x_v[:, 2:B])
+        for b in range(2, B):
             load_h(b)
 
         ident = const.tile([P, P], F32, name="ident")
@@ -97,8 +114,12 @@ def tile_tgcngraphconvolution_pa_t_kernel(tc, x, h, laplacian, weights, biases, 
         wr = wraw[:].rearrange("k (a d c o) -> k a d c o", a=2, c=2, o=2)
         gw = const.tile([P, 4 * DO], BF16, name="gw", align_bytes=64)
         gw_v = gw[:].rearrange("p (n t) -> p n t", t=4)
+        wcodes = const.tile([P, DO], U32, name="wcodes", align_bytes=64)
+        wplane = const.tile([P, DO], U8, name="wplane", align_bytes=64)
+        bias2 = const.tile([P, 512], F32, name="bias2")
+        wpss = []
         for a in range(2):
-            wps = pso.tile([P, 512], F32, tag="o", name="wps")
+            wps = o_bank()
             for s in range(2):
                 for c in range(2):
                     nc.tensor.matmul(
@@ -108,51 +129,70 @@ def tile_tgcngraphconvolution_pa_t_kernel(tc, x, h, laplacian, weights, biases, 
                         start=(c == 0),
                         stop=(c == 1),
                     )
-            nc.scalar.copy(
-                out=gw_v[:, :, 2 * a : 2 * a + 2], in_=wps[:].rearrange("p (t n) -> p n t", t=2)
-            )
-        wcodes = const.tile([P, DO], U32, name="wcodes", align_bytes=64)
-        wplane = const.tile([P, DO], U8, name="wplane", align_bytes=64)
-        nc.vector.quantize_mx(out=wcodes[:].bitcast(FP8X4), scales=wplane[:], in_=gw[:])
-
-        bps = pso.tile([P, 512], F32, tag="o", name="bps")
+            wpss.append(wps)
+        bps = o_bank()
         for s in range(2):
             nc.tensor.matmul(
                 out=bps[:, DO * s : DO * s + DO], lhsT=ones[:], rhs=brow[:], start=True, stop=True
             )
-        bias2 = const.tile([P, 512], F32, name="bias2")
-        nc.scalar.copy(out=bias2[:], in_=bps[:])
+
+        def wcopy(a):
+            nc.vector.tensor_copy(
+                out=gw_v[:, :, 2 * a : 2 * a + 2],
+                in_=wpss[a][:].rearrange("p (t n) -> p n t", t=2),
+            )
 
         xv = xraw[:].rearrange("p (b g j c) -> p b g j c", b=B, g=G, j=4)
-        xq = {}
+        xt = {}
 
-        def xh_prep(b):
-            hv = hraws[b][:].rearrange("p (g r) -> p g r", g=G)[:, :, 0 : 4 * H].rearrange(
+        def x_tiles(b):
+            if b not in xt:
+                xg = xpool.tile([P, G * F * 4], BF16, tag="xg", name="xg", align_bytes=64)
+                xcodes = xpool.tile([P, G * F], U32, tag="xcodes", name="xcodes", align_bytes=64)
+                xplane = xpool.tile([P, G * F], U8, tag="xplane", name="xplane", align_bytes=64)
+                xt[b] = (xg, xcodes, xplane)
+            return xt[b]
+
+        def h_view(b):
+            return hraws[b][:].rearrange("p (g r) -> p g r", g=G)[:, :, 0 : 4 * H].rearrange(
                 "p g (j f) -> p g j f", j=4
             )
-            xg = xpool.tile([P, G * F * 4], BF16, tag="xg", name="xg", align_bytes=64)
-            xg_v = xg[:].rearrange("p (g f j) -> p g f j", g=G, j=4)
-            xcodes = xpool.tile([P, G * F], U32, tag="xcodes", name="xcodes", align_bytes=64)
-            xplane = xpool.tile([P, G * F], U8, tag="xplane", name="xplane", align_bytes=64)
-            nc.scalar.copy(out=xg_v[:, :, 0:2, :], in_=xv[:, b].rearrange("p g j c -> p g c j"))
-            for g in range(G):
-                regroup(nc.scalar.copy, xg_v[:, g, 2:FS, :], hv[:, g, :, 0 : FS - 2], 2)
-                regroup(nc.vector.tensor_copy, xg_v[:, g, FS:F, :], hv[:, g, :, FS - 2 : H], 4)
-            for g in range(G):
-                nc.vector.quantize_mx(
-                    out=xcodes[:, F * g : F * g + F].bitcast(FP8X4),
-                    scales=xplane[:, F * g : F * g + F],
-                    in_=xg[:, 4 * F * g : 4 * F * g + 4 * F],
-                )
-            xq[b] = (xcodes, xplane)
 
-        xh_prep(0)
+        def r_scalar(q):
+            if q >= NH:
+                return
+            b, g = q // G, q % G
+            xg_v = x_tiles(b)[0][:].rearrange("p (g f j) -> p g f j", g=G, j=4)
+            nc.scalar.copy(out=xg_v[:, g, 0:2, :], in_=xv[:, b, g].rearrange("p j c -> p c j"))
+            regroup(nc.scalar.copy, xg_v[:, g, 2 : FSQ[q], :], h_view(b)[:, g, :, 0 : FSQ[q] - 2], 2)
+
+        def r_vector(q):
+            if q >= NH:
+                return
+            b, g = q // G, q % G
+            xg_v = x_tiles(b)[0][:].rearrange("p (g f j) -> p g f j", g=G, j=4)
+            regroup(
+                nc.vector.tensor_copy, xg_v[:, g, FSQ[q] : F, :], h_view(b)[:, g, :, FSQ[q] - 2 : H], 4
+            )
+
+        def q_x(q):
+            if q >= NH:
+                return
+            b, g = q // G, q % G
+            xg, xcodes, xplane = x_tiles(b)
+            nc.vector.quantize_mx(
+                out=xcodes[:, F * g : F * g + F].bitcast(FP8X4),
+                scales=xplane[:, F * g : F * g + F],
+                in_=xg[:, 4 * F * g : 4 * F * g + 4 * F],
+            )
 
         lcodes = const.tile([P, MT * G * P], U32, name="lcodes", align_bytes=64)
         lplane = const.tile([P, MT * G * P], U8, name="lplane", align_bytes=64)
-        for i in range(MT):
+        lgrps = []
+
+        def lap_t(i):
             lw = lraws[i // 2][:].bitcast(F32)[:, 512 * (i % 2) : 512 * (i % 2) + 512]
-            lps = psa.tile([P, 512], F32, tag="a", name="lps")
+            lps = a_bank()
             for q in range(4):
                 nc.tensor.transpose(lps[:, P * q : P * q + P], lw[:, P * q : P * q + P], ident[:])
             lgrp = lgpool.tile([P, N], BF16, tag="lgrp", name="lgrp", align_bytes=64)
@@ -160,20 +200,30 @@ def tile_tgcngraphconvolution_pa_t_kernel(tc, x, h, laplacian, weights, biases, 
                 out=lgrp[:].bitcast(F32).rearrange("p (g m u) -> p g m u", g=G, u=2),
                 in_=lps[:].rearrange("p (g u m) -> p g m u", g=G, u=2),
             )
+            lgrps.append(lgrp)
+
+        def lap_q(i):
             nc.vector.quantize_mx(
                 out=lcodes[:, 256 * i : 256 * i + 256].bitcast(FP8X4),
                 scales=lplane[:, 256 * i : 256 * i + 256],
-                in_=lgrp[:],
+                in_=lgrps[i][:],
             )
 
-        aq = {}
+        at = {}
 
-        def step2(b, hf):
-            xcodes, xplane = xq[b]
-            ag = apool.tile([P, 2048], BF16, tag="ag", name="ag", align_bytes=64)
-            for ii in range(4):
+        def step2(k, tiles):
+            b, hf = k // 2, k % 2
+            xcodes, xplane = x_tiles(b)[1:]
+            if k not in at:
+                ag = apool.tile([P, 2048], BF16, tag="ag", name="ag", align_bytes=64)
+                acodes = apool.tile([P, 512], U32, tag="acodes", name="acodes", align_bytes=64)
+                aplane = apool.tile([P, 512], U8, tag="aplane", name="aplane", align_bytes=64)
+                osb = opool.tile([P, 1024], F32, tag="osb", name="osb")
+                at[k] = (ag, acodes, aplane, osb)
+            ag = at[k][0]
+            for ii in tiles:
                 i = 4 * hf + ii
-                aps = psa.tile([P, 512], F32, tag="a", name="aps")
+                aps = a_bank()
                 for t in range(4):
                     for g in range(G):
                         xs = slice(F * g + P * t, F * g + P * t + P)
@@ -191,37 +241,94 @@ def tile_tgcngraphconvolution_pa_t_kernel(tc, x, h, laplacian, weights, biases, 
                     out=ag[:, 512 * ii : 512 * ii + 512].rearrange("p (m t) -> p m t", t=4),
                     in_=aps[:].rearrange("p (t m) -> p m t", t=4),
                 )
-            acodes = apool.tile([P, 512], U32, tag="acodes", name="acodes", align_bytes=64)
-            aplane = apool.tile([P, 512], U8, tag="aplane", name="aplane", align_bytes=64)
-            nc.vector.quantize_mx(out=acodes[:].bitcast(FP8X4), scales=aplane[:], in_=ag[:])
-            aq[(b, hf)] = (acodes, aplane)
 
-        def step3(b, hf):
-            acodes, aplane = aq[(b, hf)]
-            osb = opool.tile([P, 1024], F32, tag="osb", name="osb")
-            for pr in range(2):
-                ops = pso.tile([P, 512], F32, tag="o", name="ops")
-                for s in range(2):
-                    cs = slice(P * (2 * pr + s), P * (2 * pr + s) + P)
-                    nc.tensor.matmul_mx(
-                        out=ops[:, DO * s : DO * s + DO],
-                        lhsT=acodes[:, cs].bitcast(FP8X4),
-                        lhsT_scale=aplane[:, cs],
-                        rhs=wcodes[:].bitcast(FP8X4),
-                        rhs_scale=wplane[:],
-                        start=True,
-                        stop=True,
-                    )
-                nc.vector.tensor_tensor(
-                    out=osb[:, 512 * pr : 512 * pr + 512], in0=ops[:], in1=bias2[:], op=ADD
+        def q_a(k, lo, hi):
+            ag, acodes, aplane = at[k][0:3]
+            nc.vector.quantize_mx(
+                out=acodes[:, P * lo : P * hi].bitcast(FP8X4),
+                scales=aplane[:, P * lo : P * hi],
+                in_=ag[:, 512 * lo : 512 * hi],
+            )
+
+        def step3(k, pr):
+            acodes, aplane, osb = at[k][1:]
+            ops = o_bank()
+            for s in range(2):
+                cs = slice(P * (2 * pr + s), P * (2 * pr + s) + P)
+                nc.tensor.matmul_mx(
+                    out=ops[:, DO * s : DO * s + DO],
+                    lhsT=acodes[:, cs].bitcast(FP8X4),
+                    lhsT_scale=aplane[:, cs],
+                    rhs=wcodes[:].bitcast(FP8X4),
+                    rhs_scale=wplane[:],
+                    start=True,
+                    stop=True,
                 )
-            nc.sync.dma_start(out=out_v[b][:, 1024 * hf : 1024 * hf + 1024], in_=osb[:])
+            nc.vector.tensor_tensor(
+                out=osb[:, 512 * pr : 512 * pr + 512], in0=ops[:], in1=bias2[:], op=ADD
+            )
 
-        halves = [(b, hf) for b in range(B) for hf in range(2)]
-        for k, (b, hf) in enumerate(halves):
-            step2(b, hf)
-            if hf == 0 and b + 1 < B:
-                xh_prep(b + 1)
-            if k >= 1:
-                step3(*halves[k - 1])
-        step3(*halves[-1])
+        def store(k, lo, hi):
+            b, hf = k // 2, k % 2
+            nc.sync.dma_start(
+                out=out_v[b][:, 1024 * hf + 512 * lo : 1024 * hf + 512 * hi],
+                in_=at[k][3][:, 512 * lo : 512 * hi],
+            )
+
+        def step3_all(k):
+            step3(k, 0)
+            step3(k, 1)
+            store(k, 0, 2)
+
+        r_scalar(0)
+        r_vector(0)
+        r_scalar(1)
+        r_vector(1)
+        q_x(0)
+        wcopy(0)
+        q_x(1)
+        for i in range(MT):
+            lap_t(i)
+        lap_q(0)
+        lap_q(1)
+        wcopy(1)
+        lap_q(2)
+        lap_q(3)
+        nc.vector.quantize_mx(out=wcodes[:].bitcast(FP8X4), scales=wplane[:], in_=gw[:])
+        lap_q(4)
+        lap_q(5)
+        nc.vector.tensor_copy(out=bias2[:], in_=bps[:])
+        r_scalar(2)
+        r_vector(2)
+        lap_q(6)
+        lap_q(7)
+        r_scalar(3)
+        r_vector(3)
+        q_x(2)
+
+        for k in range(NH - 2):
+            step2(k, range(4))
+            if k >= 2:
+                step3_all(k - 2)
+            r_scalar(k + 4)
+            q_x(k + 3)
+            q_a(k, 0, 4)
+            r_vector(k + 4)
+
+        k = NH - 2
+        step2(k, range(0, 2))
+        step3_all(k - 2)
+        step2(k, range(2, 4))
+        q_a(k, 0, 4)
+        step3_all(k - 1)
+
+        k = NH - 1
+        step2(k, range(0, 2))
+        q_a(k, 0, 2)
+        step3_all(k - 1)
+        step2(k, range(2, 4))
+        q_a(k, 2, 4)
+        step3(k, 0)
+        store(k, 0, 1)
+        step3(k, 1)
+        store(k, 1, 2)

@@ -22,7 +22,9 @@ MT = 8
 NA = 5
 NO = 3
 NH = 2 * B
-FSQ = [176,176,32,32,96,96,176,176,176,176,176,176,176,176,176,176]
+FSQ = [112,112,32,32,64,64,112,112,112,112,112,112,112,112,112,112]
+FG = 192
+MULT = mybir.AluOpType.mult
 
 FLOPS = 2 * B * N * N * F + 2 * B * N * F * DO
 
@@ -171,9 +173,17 @@ def tile_tgcngraphconvolution_pa_t_kernel(tc, x, h, laplacian, weights, biases, 
                 return
             b, g = q // G, q % G
             xg_v = x_tiles(b)[0][:].rearrange("p (g f j) -> p g f j", g=G, j=4)
-            regroup(
-                nc.vector.tensor_copy, xg_v[:, g, FSQ[q] : F, :], h_view(b)[:, g, :, FSQ[q] - 2 : H], 4
-            )
+            for lo in (FSQ[q], FSQ[q] + FG // 2):
+                nc.gpsimd.tensor_scalar(
+                    out=xg_v[:, g, lo : lo + FG // 2, :],
+                    in0=h_view(b)[:, g, :, lo - 2 : lo - 2 + FG // 2].rearrange("p j f -> p f j"),
+                    scalar1=1.0,
+                    scalar2=0.0,
+                    op0=MULT,
+                    op1=ADD,
+                )
+            v0 = FSQ[q] + FG
+            regroup(nc.vector.tensor_copy, xg_v[:, g, v0:F, :], h_view(b)[:, g, :, v0 - 2 : H], 4)
 
         def q_x(q):
             if q >= NH:

@@ -22,9 +22,8 @@ MT = 8
 NA = 5
 NO = 3
 NH = 2 * B
-FSQ = [112,112,32,32,64,64,112,112,112,112,112,112,112,112,112,112]
-FG = 192
-MULT = mybir.AluOpType.mult
+WARM = 2
+FSQ = [176,176,32,32,96,96,176,176,176,176,176,176,176,176,176,176]
 
 FLOPS = 2 * B * N * N * F + 2 * B * N * F * DO
 
@@ -63,15 +62,15 @@ def tile_tgcngraphconvolution_pa_t_kernel(tc, x, h, laplacian, weights, biases, 
             return pso.tile([P, 512], F32, tag="o%d" % (n % NO), name="o%d" % (n % NO))
 
         h_v = h.rearrange("b (a p r) f -> b p a (r f)", a=4, r=2)
-        x_v = x.rearrange("b (a p r) c -> p b a (r c)", a=4, r=2)
+        x_v = x.rearrange("b (a r) c -> (b a) (r c)", a=4)
         lap_v = laplacian.rearrange("(r i) n -> r (i n)", i=MT)
         w_v = weights.rearrange("(a k) d c o -> k a (d c o)", a=2)
         b_v = biases.rearrange("(a d) o -> a (d o)", a=1)
         out_v = out.rearrange("b (p r) o -> b p (r o)", p=P)
 
-        xraw = const.tile([P, B * 16], BF16, name="xraw")
-        xr = xraw[:].rearrange("p (b a s) -> p b a s", b=B, a=4)
-        nc.scalar.dma_start(out=xr[:, 0:2], in_=x_v[:, 0:2])
+        xrow = const.tile([P, 512], BF16, name="xrow")
+        nc.vector.memset(xrow[:], 0.0)
+        nc.scalar.dma_start(out=xrow[0 : 4 * B, :], in_=x_v)
         wraw = const.tile([P, 1024], BF16, name="wraw")
         nc.scalar.dma_start(out=wraw[:].rearrange("k (a r) -> k a r", a=2), in_=w_v)
         brow = const.tile([P, DO], BF16, name="brow")
@@ -95,9 +94,7 @@ def tile_tgcngraphconvolution_pa_t_kernel(tc, x, h, laplacian, weights, biases, 
             lraw = lpool.tile([P, 2 * N], BF16, tag="lraw", name="lraw")
             nc.sync.dma_start(out=lraw[:], in_=lap_v[:, 2 * N * i2 : 2 * N * i2 + 2 * N])
             lraws.append(lraw)
-        load_h(1)
-        nc.sync.dma_start(out=xr[:, 2:B], in_=x_v[:, 2:B])
-        for b in range(2, B):
+        for b in range(1, B):
             load_h(b)
 
         ident = const.tile([P, P], F32, name="ident")
@@ -112,6 +109,16 @@ def tile_tgcngraphconvolution_pa_t_kernel(tc, x, h, laplacian, weights, biases, 
         perm_r = perm[:].rearrange("k (s c q) -> k s c q", s=2, c=2)
         ones = const.tile([P, P], BF16, name="ones")
         nc.vector.memset(ones[:], 1.0)
+
+        xraw = const.tile([P, B * 16], BF16, name="xraw")
+        xps = a_bank()
+        xw = xrow[:].bitcast(F32).rearrange("q (p e) -> q p e", e=2)
+        for e in range(2):
+            nc.tensor.transpose(xps[:, P * e : P * e + P], xw[:, :, e], ident[:])
+        nc.scalar.copy(
+            out=xraw[:].bitcast(F32).rearrange("p (q e) -> p q e", e=2),
+            in_=xps[:, 0 : 2 * P].rearrange("p (e q) -> p q e", e=2)[:, 0 : 4 * B, :],
+        )
 
         wr = wraw[:].rearrange("k (a d c o) -> k a d c o", a=2, c=2, o=2)
         gw = const.tile([P, 4 * DO], BF16, name="gw", align_bytes=64)
@@ -133,10 +140,16 @@ def tile_tgcngraphconvolution_pa_t_kernel(tc, x, h, laplacian, weights, biases, 
                     )
             wpss.append(wps)
         bps = o_bank()
-        for s in range(2):
-            nc.tensor.matmul(
-                out=bps[:, DO * s : DO * s + DO], lhsT=ones[:], rhs=brow[:], start=True, stop=True
-            )
+
+        def warm(n):
+            for w in range(n):
+                nc.tensor.matmul(out=bps[:], lhsT=ones[:], rhs=perm[:], start=True, stop=True)
+
+        def bias_mm():
+            for s in range(2):
+                nc.tensor.matmul(
+                    out=bps[:, DO * s : DO * s + DO], lhsT=ones[:], rhs=brow[:], start=True, stop=True
+                )
 
         def wcopy(a):
             nc.vector.tensor_copy(
@@ -173,17 +186,9 @@ def tile_tgcngraphconvolution_pa_t_kernel(tc, x, h, laplacian, weights, biases, 
                 return
             b, g = q // G, q % G
             xg_v = x_tiles(b)[0][:].rearrange("p (g f j) -> p g f j", g=G, j=4)
-            for lo in (FSQ[q], FSQ[q] + FG // 2):
-                nc.gpsimd.tensor_scalar(
-                    out=xg_v[:, g, lo : lo + FG // 2, :],
-                    in0=h_view(b)[:, g, :, lo - 2 : lo - 2 + FG // 2].rearrange("p j f -> p f j"),
-                    scalar1=1.0,
-                    scalar2=0.0,
-                    op0=MULT,
-                    op1=ADD,
-                )
-            v0 = FSQ[q] + FG
-            regroup(nc.vector.tensor_copy, xg_v[:, g, v0:F, :], h_view(b)[:, g, :, v0 - 2 : H], 4)
+            regroup(
+                nc.vector.tensor_copy, xg_v[:, g, FSQ[q] : F, :], h_view(b)[:, g, :, FSQ[q] - 2 : H], 4
+            )
 
         def q_x(q):
             if q >= NH:
@@ -298,7 +303,10 @@ def tile_tgcngraphconvolution_pa_t_kernel(tc, x, h, laplacian, weights, biases, 
         wcopy(0)
         q_x(1)
         for i in range(MT):
+            if i % 2 == 0:
+                warm(WARM)
             lap_t(i)
+        bias_mm()
         lap_q(0)
         lap_q(1)
         wcopy(1)
@@ -307,17 +315,18 @@ def tile_tgcngraphconvolution_pa_t_kernel(tc, x, h, laplacian, weights, biases, 
         nc.vector.quantize_mx(out=wcodes[:].bitcast(FP8X4), scales=wplane[:], in_=gw[:])
         lap_q(4)
         lap_q(5)
-        nc.vector.tensor_copy(out=bias2[:], in_=bps[:])
         r_scalar(2)
         r_vector(2)
         lap_q(6)
         lap_q(7)
+        step2(0, range(0, 2))
         r_scalar(3)
         r_vector(3)
         q_x(2)
+        nc.vector.tensor_copy(out=bias2[:], in_=bps[:])
 
         for k in range(NH - 2):
-            step2(k, range(4))
+            step2(k, range(2, 4) if k == 0 else range(4))
             if k >= 2:
                 step3_all(k - 2)
             r_scalar(k + 4)

@@ -22,7 +22,7 @@ MT = 8
 NA = 5
 NO = 3
 NH = 2 * B
-WARM = 2
+WARM = 1
 FSQ = [176,176,32,32,96,96,176,176,176,176,176,176,176,176,176,176]
 
 FLOPS = 2 * B * N * N * F + 2 * B * N * F * DO
@@ -69,8 +69,9 @@ def tile_tgcngraphconvolution_pa_t_kernel(tc, x, h, laplacian, weights, biases, 
         out_v = out.rearrange("b (p r) o -> b p (r o)", p=P)
 
         xrow = const.tile([P, 512], BF16, name="xrow")
-        nc.vector.memset(xrow[:], 0.0)
         nc.scalar.dma_start(out=xrow[0 : 4 * B, :], in_=x_v)
+        nc.vector.memset(xrow[32:64, :], 0.0)
+        nc.vector.memset(xrow[64:128, :], 0.0)
         wraw = const.tile([P, 1024], BF16, name="wraw")
         nc.scalar.dma_start(out=wraw[:].rearrange("k (a r) -> k a r", a=2), in_=w_v)
         brow = const.tile([P, DO], BF16, name="brow")
@@ -115,10 +116,6 @@ def tile_tgcngraphconvolution_pa_t_kernel(tc, x, h, laplacian, weights, biases, 
         xw = xrow[:].bitcast(F32).rearrange("q (p e) -> q p e", e=2)
         for e in range(2):
             nc.tensor.transpose(xps[:, P * e : P * e + P], xw[:, :, e], ident[:])
-        nc.scalar.copy(
-            out=xraw[:].bitcast(F32).rearrange("p (q e) -> p q e", e=2),
-            in_=xps[:, 0 : 2 * P].rearrange("p (e q) -> p q e", e=2)[:, 0 : 4 * B, :],
-        )
 
         wr = wraw[:].rearrange("k (a d c o) -> k a d c o", a=2, c=2, o=2)
         gw = const.tile([P, 4 * DO], BF16, name="gw", align_bytes=64)
@@ -173,13 +170,21 @@ def tile_tgcngraphconvolution_pa_t_kernel(tc, x, h, laplacian, weights, biases, 
                 "p g (j f) -> p g j f", j=4
             )
 
-        def r_scalar(q):
-            if q >= NH:
-                return
+        def r_scalar_x(q):
             b, g = q // G, q % G
             xg_v = x_tiles(b)[0][:].rearrange("p (g f j) -> p g f j", g=G, j=4)
             nc.scalar.copy(out=xg_v[:, g, 0:2, :], in_=xv[:, b, g].rearrange("p j c -> p c j"))
+
+        def r_scalar_h(q):
+            b, g = q // G, q % G
+            xg_v = x_tiles(b)[0][:].rearrange("p (g f j) -> p g f j", g=G, j=4)
             regroup(nc.scalar.copy, xg_v[:, g, 2 : FSQ[q], :], h_view(b)[:, g, :, 0 : FSQ[q] - 2], 2)
+
+        def r_scalar(q):
+            if q >= NH:
+                return
+            r_scalar_x(q)
+            r_scalar_h(q)
 
         def r_vector(q):
             if q >= NH:
@@ -295,24 +300,31 @@ def tile_tgcngraphconvolution_pa_t_kernel(tc, x, h, laplacian, weights, biases, 
             step3(k, 1)
             store(k, 0, 2)
 
-        r_scalar(0)
+        r_scalar_h(0)
         r_vector(0)
-        r_scalar(1)
+        r_scalar_h(1)
         r_vector(1)
-        q_x(0)
+        nc.scalar.copy(
+            out=xraw[:].bitcast(F32).rearrange("p (q e) -> p q e", e=2),
+            in_=xps[:, 0 : 2 * P].rearrange("p (e q) -> p q e", e=2)[:, 0 : 4 * B, :],
+        )
+        r_scalar_x(0)
+        r_scalar_x(1)
         wcopy(0)
+        q_x(0)
+        wcopy(1)
         q_x(1)
         for i in range(MT):
-            if i % 2 == 0:
+            if i % 2 == 0 and i < MT - 2:
                 warm(WARM)
+            if i == MT - 2:
+                bias_mm()
             lap_t(i)
-        bias_mm()
         lap_q(0)
         lap_q(1)
-        wcopy(1)
+        nc.vector.quantize_mx(out=wcodes[:].bitcast(FP8X4), scales=wplane[:], in_=gw[:])
         lap_q(2)
         lap_q(3)
-        nc.vector.quantize_mx(out=wcodes[:].bitcast(FP8X4), scales=wplane[:], in_=gw[:])
         lap_q(4)
         lap_q(5)
         r_scalar(2)

@@ -41,7 +41,7 @@ def tile_tgcngraphconvolution_pa_t_kernel(tc, x, h, laplacian, weights, biases, 
         const = ctx.enter_context(tc.tile_pool(name="const", bufs=1))
         hpool = ctx.enter_context(tc.tile_pool(name="hpool", bufs=8))
         lpool = ctx.enter_context(tc.tile_pool(name="lpool", bufs=4))
-        lgpool = ctx.enter_context(tc.tile_pool(name="lgpool", bufs=3))
+        lgpool = ctx.enter_context(tc.tile_pool(name="lgpool", bufs=4))
         xpool = ctx.enter_context(tc.tile_pool(name="xpool", bufs=3))
         apool = ctx.enter_context(tc.tile_pool(name="apool", bufs=4))
         opool = ctx.enter_context(tc.tile_pool(name="opool", bufs=6))
@@ -295,6 +295,28 @@ def tile_tgcngraphconvolution_pa_t_kernel(tc, x, h, laplacian, weights, biases, 
                 in_=at[k][3][:, 512 * lo : 512 * hi],
             )
 
+        def step3_tile(k, t):
+            b, hf = k // 2, k % 2
+            acodes, aplane, osb = at[k][1:]
+            ops = o_bank()
+            cs = slice(P * t, P * t + P)
+            nc.tensor.matmul_mx(
+                out=ops[:, 0:DO],
+                lhsT=acodes[:, cs].bitcast(FP8X4),
+                lhsT_scale=aplane[:, cs],
+                rhs=wcodes[:].bitcast(FP8X4),
+                rhs_scale=wplane[:],
+                start=True,
+                stop=True,
+            )
+            nc.vector.tensor_tensor(
+                out=osb[:, DO * t : DO * t + DO], in0=ops[:, 0:DO], in1=bias2[:, 0:DO], op=ADD
+            )
+            nc.sync.dma_start(
+                out=out_v[b][:, 1024 * hf + DO * t : 1024 * hf + DO * t + DO],
+                in_=osb[:, DO * t : DO * t + DO],
+            )
+
         def step3_all(k):
             step3(k, 0)
             step3(k, 1)
@@ -349,17 +371,22 @@ def tile_tgcngraphconvolution_pa_t_kernel(tc, x, h, laplacian, weights, biases, 
         k = NH - 2
         step2(k, range(0, 2))
         step3_all(k - 2)
+        q_a(k, 0, 2)
         step2(k, range(2, 4))
-        q_a(k, 0, 4)
         step3_all(k - 1)
+        q_a(k, 2, 4)
 
         k = NH - 1
         step2(k, range(0, 2))
+        step3(k - 1, 0)
         q_a(k, 0, 2)
-        step3_all(k - 1)
-        step2(k, range(2, 4))
-        q_a(k, 2, 4)
+        step2(k, range(2, 3))
+        step3(k - 1, 1)
+        store(k - 1, 0, 2)
+        q_a(k, 2, 3)
+        step2(k, range(3, 4))
         step3(k, 0)
         store(k, 0, 1)
-        step3(k, 1)
-        store(k, 1, 2)
+        q_a(k, 3, 4)
+        step3_tile(k, 2)
+        step3_tile(k, 3)

@@ -23,7 +23,9 @@ NA = 5
 NO = 3
 NH = 2 * B
 WARM = 1
-FSQ = [176,176,32,32,96,96,176,176,176,176,176,176,176,176,176,176]
+FSQ = [176,176,32,32,96,96,128,128,128,128,128,128,128,128,128,128]
+FGQ = [0,0,0,0,0,0,160,160,160,160,160,160,160,160,160,160]
+MULT = mybir.AluOpType.mult
 
 FLOPS = 2 * B * N * N * F + 2 * B * N * F * DO
 
@@ -43,6 +45,7 @@ def tile_tgcngraphconvolution_pa_t_kernel(tc, x, h, laplacian, weights, biases, 
         lpool = ctx.enter_context(tc.tile_pool(name="lpool", bufs=4))
         lgpool = ctx.enter_context(tc.tile_pool(name="lgpool", bufs=4))
         xpool = ctx.enter_context(tc.tile_pool(name="xpool", bufs=3))
+        xgpool = ctx.enter_context(tc.tile_pool(name="xgpool", bufs=2))
         apool = ctx.enter_context(tc.tile_pool(name="apool", bufs=4))
         opool = ctx.enter_context(tc.tile_pool(name="opool", bufs=6))
         psa = ctx.enter_context(tc.psum_pool(name="psa", bufs=1))
@@ -157,13 +160,22 @@ def tile_tgcngraphconvolution_pa_t_kernel(tc, x, h, laplacian, weights, biases, 
         xv = xraw[:].rearrange("p (b g j c) -> p b g j c", b=B, g=G, j=4)
         xt = {}
 
+        xgt = {}
+
         def x_tiles(b):
             if b not in xt:
-                xg = xpool.tile([P, G * F * 4], BF16, tag="xg", name="xg", align_bytes=64)
                 xcodes = xpool.tile([P, G * F], U32, tag="xcodes", name="xcodes", align_bytes=64)
                 xplane = xpool.tile([P, G * F], U8, tag="xplane", name="xplane", align_bytes=64)
-                xt[b] = (xg, xcodes, xplane)
+                xt[b] = (None, xcodes, xplane)
             return xt[b]
+
+        def xg_tile(q):
+            if q not in xgt:
+                xgt[q] = xgpool.tile([P, F * 4], BF16, tag="xg", name="xg", align_bytes=64)
+            return xgt[q]
+
+        def xg_view(q):
+            return xg_tile(q)[:].rearrange("p (f j) -> p f j", j=4)
 
         def h_view(b):
             return hraws[b][:].rearrange("p (g r) -> p g r", g=G)[:, :, 0 : 4 * H].rearrange(
@@ -172,13 +184,11 @@ def tile_tgcngraphconvolution_pa_t_kernel(tc, x, h, laplacian, weights, biases, 
 
         def r_scalar_x(q):
             b, g = q // G, q % G
-            xg_v = x_tiles(b)[0][:].rearrange("p (g f j) -> p g f j", g=G, j=4)
-            nc.scalar.copy(out=xg_v[:, g, 0:2, :], in_=xv[:, b, g].rearrange("p j c -> p c j"))
+            nc.scalar.copy(out=xg_view(q)[:, 0:2, :], in_=xv[:, b, g].rearrange("p j c -> p c j"))
 
         def r_scalar_h(q):
             b, g = q // G, q % G
-            xg_v = x_tiles(b)[0][:].rearrange("p (g f j) -> p g f j", g=G, j=4)
-            regroup(nc.scalar.copy, xg_v[:, g, 2 : FSQ[q], :], h_view(b)[:, g, :, 0 : FSQ[q] - 2], 2)
+            regroup(nc.scalar.copy, xg_view(q)[:, 2 : FSQ[q], :], h_view(b)[:, g, :, 0 : FSQ[q] - 2], 2)
 
         def r_scalar(q):
             if q >= NH:
@@ -190,20 +200,32 @@ def tile_tgcngraphconvolution_pa_t_kernel(tc, x, h, laplacian, weights, biases, 
             if q >= NH:
                 return
             b, g = q // G, q % G
-            xg_v = x_tiles(b)[0][:].rearrange("p (g f j) -> p g f j", g=G, j=4)
-            regroup(
-                nc.vector.tensor_copy, xg_v[:, g, FSQ[q] : F, :], h_view(b)[:, g, :, FSQ[q] - 2 : H], 4
+            v0 = FSQ[q] + FGQ[q]
+            regroup(nc.vector.tensor_copy, xg_view(q)[:, v0:F, :], h_view(b)[:, g, :, v0 - 2 : H], 4)
+
+        def r_gpsimd(q):
+            if q >= NH or FGQ[q] == 0:
+                return
+            b, g = q // G, q % G
+            lo, hi = FSQ[q], FSQ[q] + FGQ[q]
+            nc.gpsimd.tensor_scalar(
+                out=xg_view(q)[:, lo:hi, :],
+                in0=h_view(b)[:, g, :, lo - 2 : hi - 2].rearrange("p j f -> p f j"),
+                scalar1=1.0,
+                scalar2=0.0,
+                op0=MULT,
+                op1=ADD,
             )
 
         def q_x(q):
             if q >= NH:
                 return
             b, g = q // G, q % G
-            xg, xcodes, xplane = x_tiles(b)
+            xcodes, xplane = x_tiles(b)[1:]
             nc.vector.quantize_mx(
                 out=xcodes[:, F * g : F * g + F].bitcast(FP8X4),
                 scales=xplane[:, F * g : F * g + F],
-                in_=xg[:, 4 * F * g : 4 * F * g + 4 * F],
+                in_=xg_tile(q)[:],
             )
 
         lcodes = const.tile([P, MT * G * P], U32, name="lcodes", align_bytes=64)
@@ -364,6 +386,7 @@ def tile_tgcngraphconvolution_pa_t_kernel(tc, x, h, laplacian, weights, biases, 
             if k >= 2:
                 step3_all(k - 2)
             r_scalar(k + 4)
+            r_gpsimd(k + 4)
             q_x(k + 3)
             q_a(k, 0, 4)
             r_vector(k + 4)

@@ -22,10 +22,8 @@ MT = 8
 NA = 5
 NO = 3
 NH = 2 * B
-WARM = 1
-FSQ = [176,176,32,32,96,96,128,128,128,128,128,128,128,128,128,128]
-FGQ = [0,0,0,0,0,0,160,160,160,160,160,160,160,160,160,160]
-MULT = mybir.AluOpType.mult
+WARM = 0
+FSQ = [176,176,32,32,96,96,176,176,176,176,176,176,176,176,176,176]
 
 FLOPS = 2 * B * N * N * F + 2 * B * N * F * DO
 
@@ -45,7 +43,6 @@ def tile_tgcngraphconvolution_pa_t_kernel(tc, x, h, laplacian, weights, biases, 
         lpool = ctx.enter_context(tc.tile_pool(name="lpool", bufs=4))
         lgpool = ctx.enter_context(tc.tile_pool(name="lgpool", bufs=4))
         xpool = ctx.enter_context(tc.tile_pool(name="xpool", bufs=3))
-        xgpool = ctx.enter_context(tc.tile_pool(name="xgpool", bufs=2))
         apool = ctx.enter_context(tc.tile_pool(name="apool", bufs=4))
         opool = ctx.enter_context(tc.tile_pool(name="opool", bufs=6))
         psa = ctx.enter_context(tc.psum_pool(name="psa", bufs=1))
@@ -160,22 +157,13 @@ def tile_tgcngraphconvolution_pa_t_kernel(tc, x, h, laplacian, weights, biases, 
         xv = xraw[:].rearrange("p (b g j c) -> p b g j c", b=B, g=G, j=4)
         xt = {}
 
-        xgt = {}
-
         def x_tiles(b):
             if b not in xt:
+                xg = xpool.tile([P, G * F * 4], BF16, tag="xg", name="xg", align_bytes=64)
                 xcodes = xpool.tile([P, G * F], U32, tag="xcodes", name="xcodes", align_bytes=64)
                 xplane = xpool.tile([P, G * F], U8, tag="xplane", name="xplane", align_bytes=64)
-                xt[b] = (None, xcodes, xplane)
+                xt[b] = (xg, xcodes, xplane)
             return xt[b]
-
-        def xg_tile(q):
-            if q not in xgt:
-                xgt[q] = xgpool.tile([P, F * 4], BF16, tag="xg", name="xg", align_bytes=64)
-            return xgt[q]
-
-        def xg_view(q):
-            return xg_tile(q)[:].rearrange("p (f j) -> p f j", j=4)
 
         def h_view(b):
             return hraws[b][:].rearrange("p (g r) -> p g r", g=G)[:, :, 0 : 4 * H].rearrange(
@@ -184,11 +172,13 @@ def tile_tgcngraphconvolution_pa_t_kernel(tc, x, h, laplacian, weights, biases, 
 
         def r_scalar_x(q):
             b, g = q // G, q % G
-            nc.scalar.copy(out=xg_view(q)[:, 0:2, :], in_=xv[:, b, g].rearrange("p j c -> p c j"))
+            xg_v = x_tiles(b)[0][:].rearrange("p (g f j) -> p g f j", g=G, j=4)
+            nc.scalar.copy(out=xg_v[:, g, 0:2, :], in_=xv[:, b, g].rearrange("p j c -> p c j"))
 
         def r_scalar_h(q):
             b, g = q // G, q % G
-            regroup(nc.scalar.copy, xg_view(q)[:, 2 : FSQ[q], :], h_view(b)[:, g, :, 0 : FSQ[q] - 2], 2)
+            xg_v = x_tiles(b)[0][:].rearrange("p (g f j) -> p g f j", g=G, j=4)
+            regroup(nc.scalar.copy, xg_v[:, g, 2 : FSQ[q], :], h_view(b)[:, g, :, 0 : FSQ[q] - 2], 2)
 
         def r_scalar(q):
             if q >= NH:
@@ -200,32 +190,20 @@ def tile_tgcngraphconvolution_pa_t_kernel(tc, x, h, laplacian, weights, biases, 
             if q >= NH:
                 return
             b, g = q // G, q % G
-            v0 = FSQ[q] + FGQ[q]
-            regroup(nc.vector.tensor_copy, xg_view(q)[:, v0:F, :], h_view(b)[:, g, :, v0 - 2 : H], 4)
-
-        def r_gpsimd(q):
-            if q >= NH or FGQ[q] == 0:
-                return
-            b, g = q // G, q % G
-            lo, hi = FSQ[q], FSQ[q] + FGQ[q]
-            nc.gpsimd.tensor_scalar(
-                out=xg_view(q)[:, lo:hi, :],
-                in0=h_view(b)[:, g, :, lo - 2 : hi - 2].rearrange("p j f -> p f j"),
-                scalar1=1.0,
-                scalar2=0.0,
-                op0=MULT,
-                op1=ADD,
+            xg_v = x_tiles(b)[0][:].rearrange("p (g f j) -> p g f j", g=G, j=4)
+            regroup(
+                nc.vector.tensor_copy, xg_v[:, g, FSQ[q] : F, :], h_view(b)[:, g, :, FSQ[q] - 2 : H], 4
             )
 
         def q_x(q):
             if q >= NH:
                 return
             b, g = q // G, q % G
-            xcodes, xplane = x_tiles(b)[1:]
+            xg, xcodes, xplane = x_tiles(b)
             nc.vector.quantize_mx(
                 out=xcodes[:, F * g : F * g + F].bitcast(FP8X4),
                 scales=xplane[:, F * g : F * g + F],
-                in_=xg_tile(q)[:],
+                in_=xg[:, 4 * F * g : 4 * F * g + 4 * F],
             )
 
         lcodes = const.tile([P, MT * G * P], U32, name="lcodes", align_bytes=64)
@@ -386,7 +364,6 @@ def tile_tgcngraphconvolution_pa_t_kernel(tc, x, h, laplacian, weights, biases, 
             if k >= 2:
                 step3_all(k - 2)
             r_scalar(k + 4)
-            r_gpsimd(k + 4)
             q_x(k + 3)
             q_a(k, 0, 4)
             r_vector(k + 4)

from contextlib import ExitStack

import concourse.mybir as mybir
from concourse.masks import make_identity

BF16 = mybir.dt.bfloat16
F32 = mybir.dt.float32
U32 = mybir.dt.uint32
U8 = mybir.dt.uint8
FP8X4 = mybir.dt.float8_e4m3fn_x4
ADD = mybir.AluOpType.add

P = 128
B = 8
N = 1024
F = 512
H = 510
DO = 256
G = 2
HP = 2048
MT = 8
NA = 5
NO = 3
NH = 2 * B
WARM = 0
FSQ = [176,176,32,32,96,96,176,176,176,176,176,176,176,176,176,176]

FLOPS = 2 * B * N * N * F + 2 * B * N * F * DO


def regroup(copy, dst, src, run):
    copy(
        out=dst.rearrange("p (c i) j -> p c j i", i=run),
        in_=src.rearrange("p j (c i) -> p c j i", i=run),
    )


def tile_tgcngraphconvolution_pa_t_kernel(tc, x, h, laplacian, weights, biases, out):
    nc = tc.nc
    with ExitStack() as ctx:
        const = ctx.enter_context(tc.tile_pool(name="const", bufs=1))
        hpool = ctx.enter_context(tc.tile_pool(name="hpool", bufs=8))
        lpool = ctx.enter_context(tc.tile_pool(name="lpool", bufs=4))
        lgpool = ctx.enter_context(tc.tile_pool(name="lgpool", bufs=4))
        xpool = ctx.enter_context(tc.tile_pool(name="xpool", bufs=3))
        apool = ctx.enter_context(tc.tile_pool(name="apool", bufs=4))
        opool = ctx.enter_context(tc.tile_pool(name="opool", bufs=6))
        psa = ctx.enter_context(tc.psum_pool(name="psa", bufs=1))
        pso = ctx.enter_context(tc.psum_pool(name="pso", bufs=1))
        ctx.enter_context(tc.manual_schedule())

        count = {"a": 0, "o": 0}

        def a_bank():
            n = count["a"]
            count["a"] = n + 1
            return psa.tile([P, 512], F32, tag="a%d" % (n % NA), name="a%d" % (n % NA))

        def o_bank():
            n = count["o"]
            count["o"] = n + 1
            return pso.tile([P, 512], F32, tag="o%d" % (n % NO), name="o%d" % (n % NO))

        h_v = h.rearrange("b (a p r) f -> b p a (r f)", a=4, r=2)
        x_v = x.rearrange("b (a r) c -> (b a) (r c)", a=4)
        lap_v = laplacian.rearrange("(r i) n -> r (i n)", i=MT)
        w_v = weights.rearrange("(a k) d c o -> k a (d c o)", a=2)
        b_v = biases.rearrange("(a d) o -> a (d o)", a=1)
        out_v = out.rearrange("b (p r) o -> b p (r o)", p=P)

        xrow = const.tile([P, 512], BF16, name="xrow")
        nc.scalar.dma_start(out=xrow[0 : 4 * B, :], in_=x_v)
        nc.vector.memset(xrow[32:64, :], 0.0)
        nc.vector.memset(xrow[64:128, :], 0.0)
        wraw = const.tile([P, 1024], BF16, name="wraw")
        nc.scalar.dma_start(out=wraw[:].rearrange("k (a r) -> k a r", a=2), in_=w_v)
        brow = const.tile([P, DO], BF16, name="brow")
        nc.vector.memset(brow[:], 0.0)
        nc.scalar.dma_start(out=brow[0:1, :], in_=b_v)

        hraws = []
        lraws = []

        def load_h(b):
            hraw = hpool.tile([P, G * HP], BF16, tag="hraw", name="hraw")
            for g in range(G):
                nc.sync.dma_start(
                    out=hraw[:, HP * g : HP * g + 4 * H].rearrange("p (a r) -> p a r", a=2),
                    in_=h_v[b][:, 2 * g : 2 * g + 2, :],
                )
            hraws.append(hraw)

        load_h(0)
        for i2 in range(MT // 2):
            lraw = lpool.tile([P, 2 * N], BF16, tag="lraw", name="lraw")
            nc.sync.dma_start(out=lraw[:], in_=lap_v[:, 2 * N * i2 : 2 * N * i2 + 2 * N])
            lraws.append(lraw)
        for b in range(1, B):
            load_h(b)

        ident = const.tile([P, P], F32, name="ident")
        make_identity(nc, ident[:])
        perm = const.tile([P, 4 * P], BF16, name="perm")
        nc.vector.memset(perm[:], 0.0)
        perm_w = perm[:].rearrange("k (s c i e) -> k s c i e", s=2, c=2, e=2)
        for c in range(2):
            nc.vector.tensor_copy(
                out=perm_w[:, :, c, :, c], in_=ident[:].rearrange("k (s i) -> k s i", s=2)
            )
        perm_r = perm[:].rearrange("k (s c q) -> k s c q", s=2, c=2)
        ones = const.tile([P, P], BF16, name="ones")
        nc.vector.memset(ones[:], 1.0)

        xraw = const.tile([P, B * 16], BF16, name="xraw")
        xps = a_bank()
        xw = xrow[:].bitcast(F32).rearrange("q (p e) -> q p e", e=2)
        for e in range(2):
            nc.tensor.transpose(xps[:, P * e : P * e + P], xw[:, :, e], ident[:])

        wr = wraw[:].rearrange("k (a d c o) -> k a d c o", a=2, c=2, o=2)
        gw = const.tile([P, 4 * DO], BF16, name="gw", align_bytes=64)
        gw_v = gw[:].rearrange("p (n t) -> p n t", t=4)
        wcodes = const.tile([P, DO], U32, name="wcodes", align_bytes=64)
        wplane = const.tile([P, DO], U8, name="wplane", align_bytes=64)
        bias2 = const.tile([P, 512], F32, name="bias2")
        wpss = []
        for a in range(2):
            wps = o_bank()
            for s in range(2):
                for c in range(2):
                    nc.tensor.matmul(
                        out=wps[:, DO * s : DO * s + DO].rearrange("p (d o) -> p d o", o=2),
                        lhsT=perm_r[:, s, c, :],
                        rhs=wr[:, a, :, c, :],
                        start=(c == 0),
                        stop=(c == 1),
                    )
            wpss.append(wps)
        bps = o_bank()

        def warm(n):
            for w in range(n):
                nc.tensor.matmul(out=bps[:], lhsT=ones[:], rhs=perm[:], start=True, stop=True)

        def bias_mm():
            for s in range(2):
                nc.tensor.matmul(
                    out=bps[:, DO * s : DO * s + DO], lhsT=ones[:], rhs=brow[:], start=True, stop=True
                )

        def wcopy(a):
            nc.vector.tensor_copy(
                out=gw_v[:, :, 2 * a : 2 * a + 2],
                in_=wpss[a][:].rearrange("p (t n) -> p n t", t=2),
            )

        xv = xraw[:].rearrange("p (b g j c) -> p b g j c", b=B, g=G, j=4)
        xt = {}

        def x_tiles(b):
            if b not in xt:
                xg = xpool.tile([P, G * F * 4], BF16, tag="xg", name="xg", align_bytes=64)
                xcodes = xpool.tile([P, G * F], U32, tag="xcodes", name="xcodes", align_bytes=64)
                xplane = xpool.tile([P, G * F], U8, tag="xplane", name="xplane", align_bytes=64)
                xt[b] = (xg, xcodes, xplane)
            return xt[b]

        def h_view(b):
            return hraws[b][:].rearrange("p (g r) -> p g r", g=G)[:, :, 0 : 4 * H].rearrange(
                "p g (j f) -> p g j f", j=4
            )

        def r_scalar_x(q):
            b, g = q // G, q % G
            xg_v = x_tiles(b)[0][:].rearrange("p (g f j) -> p g f j", g=G, j=4)
            nc.scalar.copy(out=xg_v[:, g, 0:2, :], in_=xv[:, b, g].rearrange("p j c -> p c j"))

        def r_scalar_h(q):
            b, g = q // G, q % G
            xg_v = x_tiles(b)[0][:].rearrange("p (g f j) -> p g f j", g=G, j=4)
            regroup(nc.scalar.copy, xg_v[:, g, 2 : FSQ[q], :], h_view(b)[:, g, :, 0 : FSQ[q] - 2], 2)

        def r_scalar(q):
            if q >= NH:
                return
            r_scalar_x(q)
            r_scalar_h(q)

        def r_vector(q):
            if q >= NH:
                return
            b, g = q // G, q % G
            xg_v = x_tiles(b)[0][:].rearrange("p (g f j) -> p g f j", g=G, j=4)
            regroup(
                nc.vector.tensor_copy, xg_v[:, g, FSQ[q] : F, :], h_view(b)[:, g, :, FSQ[q] - 2 : H], 4
            )

        def q_x(q):
            if q >= NH:
                return
            b, g = q // G, q % G
            xg, xcodes, xplane = x_tiles(b)
            nc.vector.quantize_mx(
                out=xcodes[:, F * g : F * g + F].bitcast(FP8X4),
                scales=xplane[:, F * g : F * g + F],
                in_=xg[:, 4 * F * g : 4 * F * g + 4 * F],
            )

        lcodes = const.tile([P, MT * G * P], U32, name="lcodes", align_bytes=64)
        lplane = const.tile([P, MT * G * P], U8, name="lplane", align_bytes=64)
        lgrps = []

        def lap_t(i):
            lw = lraws[i // 2][:].bitcast(F32)[:, 512 * (i % 2) : 512 * (i % 2) + 512]
            lps = a_bank()
            for q in range(4):
                nc.tensor.transpose(lps[:, P * q : P * q + P], lw[:, P * q : P * q + P], ident[:])
            lgrp = lgpool.tile([P, N], BF16, tag="lgrp", name="lgrp", align_bytes=64)
            nc.scalar.copy(
                out=lgrp[:].bitcast(F32).rearrange("p (g m u) -> p g m u", g=G, u=2),
                in_=lps[:].rearrange("p (g u m) -> p g m u", g=G, u=2),
            )
            lgrps.append(lgrp)

        def lap_q(i):
            nc.vector.quantize_mx(
                out=lcodes[:, 256 * i : 256 * i + 256].bitcast(FP8X4),
                scales=lplane[:, 256 * i : 256 * i + 256],
                in_=lgrps[i][:],
            )

        at = {}

        def step2(k, tiles):
            b, hf = k // 2, k % 2
            xcodes, xplane = x_tiles(b)[1:]
            if k not in at:
                ag = apool.tile([P, 2048], BF16, tag="ag", name="ag", align_bytes=64)
                acodes = apool.tile([P, 512], U32, tag="acodes", name="acodes", align_bytes=64)
                aplane = apool.tile([P, 512], U8, tag="aplane", name="aplane", align_bytes=64)
                osb = opool.tile([P, 1024], F32, tag="osb", name="osb")
                at[k] = (ag, acodes, aplane, osb)
            ag = at[k][0]
            for ii in tiles:
                i = 4 * hf + ii
                aps = a_bank()
                for t in range(4):
                    for g in range(G):
                        xs = slice(F * g + P * t, F * g + P * t + P)
                        ls = slice(256 * i + P * g, 256 * i + P * g + P)
                        nc.tensor.matmul_mx(
                            out=aps[:, P * t : P * t + P],
                            lhsT=xcodes[:, xs].bitcast(FP8X4),
                            lhsT_scale=xplane[:, xs],
                            rhs=lcodes[:, ls].bitcast(FP8X4),
                            rhs_scale=lplane[:, ls],
                            start=(g == 0),
                            stop=(g == G - 1),
                        )
                nc.scalar.copy(
                    out=ag[:, 512 * ii : 512 * ii + 512].rearrange("p (m t) -> p m t", t=4),
                    in_=aps[:].rearrange("p (t m) -> p m t", t=4),
                )

        def q_a(k, lo, hi):
            ag, acodes, aplane = at[k][0:3]
            nc.vector.quantize_mx(
                out=acodes[:, P * lo : P * hi].bitcast(FP8X4),
                scales=aplane[:, P * lo : P * hi],
                in_=ag[:, 512 * lo : 512 * hi],
            )

        def step3(k, pr):
            acodes, aplane, osb = at[k][1:]
            ops = o_bank()
            for s in range(2):
                cs = slice(P * (2 * pr + s), P * (2 * pr + s) + P)
                nc.tensor.matmul_mx(
                    out=ops[:, DO * s : DO * s + DO],
                    lhsT=acodes[:, cs].bitcast(FP8X4),
                    lhsT_scale=aplane[:, cs],
                    rhs=wcodes[:].bitcast(FP8X4),
                    rhs_scale=wplane[:],
                    start=True,
                    stop=True,
                )
            nc.vector.tensor_tensor(
                out=osb[:, 512 * pr : 512 * pr + 512], in0=ops[:], in1=bias2[:], op=ADD
            )

        def store(k, lo, hi):
            b, hf = k // 2, k % 2
            nc.sync.dma_start(
                out=out_v[b][:, 1024 * hf + 512 * lo : 1024 * hf + 512 * hi],
                in_=at[k][3][:, 512 * lo : 512 * hi],
            )

        def step3_tile(k, t):
            b, hf = k // 2, k % 2
            acodes, aplane, osb = at[k][1:]
            ops = o_bank()
            cs = slice(P * t, P * t + P)
            nc.tensor.matmul_mx(
                out=ops[:, 0:DO],
                lhsT=acodes[:, cs].bitcast(FP8X4),
                lhsT_scale=aplane[:, cs],
                rhs=wcodes[:].bitcast(FP8X4),
                rhs_scale=wplane[:],
                start=True,
                stop=True,
            )
            nc.vector.tensor_tensor(
                out=osb[:, DO * t : DO * t + DO], in0=ops[:, 0:DO], in1=bias2[:, 0:DO], op=ADD
            )
            nc.sync.dma_start(
                out=out_v[b][:, 1024 * hf + DO * t : 1024 * hf + DO * t + DO],
                in_=osb[:, DO * t : DO * t + DO],
            )

        def step3_all(k):
            step3(k, 0)
            step3(k, 1)
            store(k, 0, 2)

        r_scalar_h(0)
        r_vector(0)
        r_scalar_h(1)
        r_vector(1)
        nc.scalar.copy(
            out=xraw[:].bitcast(F32).rearrange("p (q e) -> p q e", e=2),
            in_=xps[:, 0 : 2 * P].rearrange("p (e q) -> p q e", e=2)[:, 0 : 4 * B, :],
        )
        r_scalar_x(0)
        r_scalar_x(1)
        wcopy(0)
        q_x(0)
        wcopy(1)
        q_x(1)
        for i in range(MT):
            if i % 2 == 0 and i < MT - 2:
                warm(WARM)
            if i == MT - 2:
                bias_mm()
            lap_t(i)
        lap_q(0)
        lap_q(1)
        nc.vector.quantize_mx(out=wcodes[:].bitcast(FP8X4), scales=wplane[:], in_=gw[:])
        lap_q(2)
        lap_q(3)
        lap_q(4)
        lap_q(5)
        r_scalar(2)
        r_vector(2)
        lap_q(6)
        lap_q(7)
        step2(0, range(0, 2))
        r_scalar(3)
        r_vector(3)
        q_x(2)
        nc.vector.tensor_copy(out=bias2[:], in_=bps[:])

        for k in range(NH - 2):
            step2(k, range(2, 4) if k == 0 else range(4))
            if k >= 2:
                step3_all(k - 2)
            r_scalar(k + 4)
            q_x(k + 3)
            q_a(k, 0, 4)
            r_vector(k + 4)

        k = NH - 2
        step2(k, range(0, 2))
        step3_all(k - 2)
        q_a(k, 0, 2)
        step2(k, range(2, 4))
        step3_all(k - 1)
        q_a(k, 2, 4)

        k = NH - 1
        step2(k, range(0, 2))
        step3(k - 1, 0)
        q_a(k, 0, 2)
        step2(k, range(2, 3))
        step3(k - 1, 1)
        store(k - 1, 0, 2)
        q_a(k, 2, 3)
        step2(k, range(3, 4))
        step3(k, 0)
        store(k, 0, 1)
        q_a(k, 3, 4)
        step3_tile(k, 2)
        step3_tile(k, 3)
